import numpy as np
import ml_dtypes


BF16 = ml_dtypes.bfloat16


def bf(x):
    return np.asarray(x, np.float32).astype(BF16)


def f64(x):
    return np.asarray(x).astype(np.float64)


E2M1 = np.array([0.0, 0.5, 1.0, 1.5, 2.0, 3.0, 4.0, 6.0, -0.0, -0.5, -1.0, -1.5, -2.0, -3.0, -4.0, -6.0])


def pack_weight(w, fmt):
    k, n = w.shape
    w = f64(bf(w)).reshape(k // 32, 32, n)
    amax = np.abs(w).max(1)
    if fmt == "e4m3":
        byte = np.frexp(amax)[1] - 1 + 127 - 7
    else:
        mant, ex = np.frexp(amax / 6.0)
        byte = np.where(mant > 0.5, ex, ex - 1) + 127
    byte = np.clip(np.where(amax > 0, byte, 1), 1, 254)
    scaled = (w * np.exp2(127.0 - byte)[:, None, :]).reshape(k, n).astype(np.float32)
    by_word = np.ascontiguousarray(scaled.reshape(k // 512, 128, 4, n).transpose(0, 1, 3, 2))
    if fmt == "e4m3":
        words = by_word.astype(ml_dtypes.float8_e4m3fn).view(np.uint8)
    else:
        c = by_word.astype(ml_dtypes.float4_e2m1fn).view(np.uint8) & 0xF
        words = c[..., 0::2] | (c[..., 1::2] << 4)
    return np.ascontiguousarray(words), np.ascontiguousarray(byte.astype(np.uint8).reshape(k // 512, 16, n))


def unpack_weight(words, scales, fmt):
    g, p, n, _ = words.shape
    if fmt == "e4m3":
        vals = np.ascontiguousarray(words).view(ml_dtypes.float8_e4m3fn).astype(np.float64)
    else:
        nib = np.empty((g, p, n, 4), np.uint8)
        nib[..., 0::2] = words & 0xF
        nib[..., 1::2] = words >> 4
        vals = E2M1[nib]
    vals = vals * np.repeat(np.exp2(scales.astype(np.float64) - 127.0), 8, axis=1)[..., None]
    return vals.transpose(0, 1, 3, 2).reshape(g * 512, n)

def pack4(w):
    words, scales = pack_weight(w, "e2m1")
    return words.reshape(words.shape[0], 128, -1), scales


def unpack4(words, scales):
    return unpack_weight(words.reshape(words.shape[0], 128, -1, 2), scales, "e2m1")


def kspread(k):
    return np.exp2(np.repeat(np.random.randint(-6, 7, k // 32), 32).astype(np.float64))


F, S, D, NH, WIN = 24, 64, 4096, 16, 8
HD = D // NH
L = F * S
EPS_NORM = 1e-6
ROPE_BASE = 10000.0


def rmsnorm(h, w):
    return h / np.sqrt(np.mean(h * h, axis=-1, keepdims=True) + EPS_NORM) * w


def rope(h, cos, sin):
    hr = h[..., 0::2]
    hi = h[..., 1::2]
    c = cos[:, None, :]
    s = sin[:, None, :]
    return np.stack([hr * c - hi * s, hr * s + hi * c], axis=-1).reshape(h.shape)


def setup_inputs():
    s = kspread(D)
    half = HD // 2
    ang = np.arange(L)[:, None] * (1.0 / ROPE_BASE ** (np.arange(half) / half))[None, :]
    x = np.random.standard_normal((F, S, D)) * s
    x_words, x_scales = pack4(np.ascontiguousarray(x.reshape(L, D).T))
    proj_w = np.random.standard_normal((D, D)) / np.sqrt(D) / s[None, :]
    words, scales = pack4(np.ascontiguousarray(proj_w.T))
    return {"x_words": x_words,
            "x_scales": x_scales,
            "freqs_cos": bf(np.cos(ang)),
            "freqs_sin": bf(np.sin(ang)),
            "proj_w_words": words,
            "proj_w_scales": scales,
            "proj_b": bf(np.random.standard_normal(D) * 0.1),
            "norm_w": bf(1.0 + 0.1 * np.random.standard_normal(D))}


def reference(x_words, x_scales, freqs_cos, freqs_sin, proj_w_words, proj_w_scales, proj_b, norm_w):
    xq = unpack4(x_words, x_scales).T.reshape(F, S, D)
    h = (xq @ unpack4(proj_w_words, proj_w_scales)) + f64(proj_b)
    hn = rmsnorm(h, f64(norm_w))
    hr = rope(hn.reshape(L, NH, HD), f64(freqs_cos), f64(freqs_sin))
    return np.ascontiguousarray(hr.reshape(F, S, NH, HD).transpose(1, 0, 2, 3))

@@ -1,0 +1,250 @@
+from contextlib import ExitStack
+
+import concourse.mybir as mybir
+from concourse.masks import make_identity
+
+F32 = mybir.dt.float32
+BF16 = mybir.dt.bfloat16
+I32 = mybir.dt.int32
+U8 = mybir.dt.uint8
+FP4X4 = mybir.dt.float4_e2m1fn_x4
+ACT = mybir.ActivationFunctionType
+ALU = mybir.AluOpType
+
+FRAMES, TOKENS, D, HEADS = 24, 64, 4096, 16
+HEAD = D // HEADS
+PAIRS = HEAD // 2
+ROWS = FRAMES * TOKENS
+EPS = 1e-6
+
+P = 128
+PASSES = D // 512
+TILES = ROWS // P
+N = 512
+CHUNK = 1024
+CHUNKS = D // CHUNK
+HPC = CHUNK // HEAD
+
+FLOPS = 2 * ROWS * D * D
+
+SEGMENTS = [(0, 512), (512, 512), (1024, 1024), (2048, 1024), (3072, 1024)]
+V_CHUNKS = (1, 3)
+
+
+def tile_temporalattention_pa_kernel(
+    tc, x_words, x_scales, freqs_cos, freqs_sin, w_words, w_scales, proj_b, norm_w, out
+):
+    nc = tc.nc
+    with ExitStack() as ctx:
+        keep = ctx.enter_context(tc.tile_pool(name="keep", bufs=1))
+        work = ctx.enter_context(tc.tile_pool(name="work", bufs=2))
+        psum = ctx.enter_context(tc.psum_pool(name="psum", bufs=1))
+        ctx.enter_context(tc.manual_schedule())
+
+        x_parts = [(0, 256), (256, ROWS - 256)]
+        x_codes = [keep.tile([P, PASSES, 2 * n], U8, name=f"xc{i}", align_bytes=64) for i, (a, n) in enumerate(x_parts)]
+        x_planes = [keep.tile([P, PASSES, n], U8, name=f"xs{i}", align_bytes=64) for i, (a, n) in enumerate(x_parts)]
+        w_codes = [keep.tile([P, PASSES, 2 * n], U8, name=f"wc{i}", align_bytes=64) for i, (a, n) in enumerate(SEGMENTS)]
+        w_planes = [keep.tile([P, PASSES, n], U8, name=f"ws{i}", align_bytes=64) for i, (a, n) in enumerate(SEGMENTS)]
+
+        def load_codes(tile, words, first, count, k0, k1):
+            nc.sync.dma_start(
+                out=tile[:, k0:k1, :].bitcast(I32),
+                in_=words[k0:k1, :, 2 * first : 2 * (first + count)].rearrange("g p n -> p g n").bitcast(I32),
+            )
+
+        def load_scales(tile, scales, first, count):
+            for q in range(4):
+                nc.sync.dma_start(
+                    out=tile[32 * q : 32 * q + 4, :, :].bitcast(I32),
+                    in_=scales[:, 4 * q : 4 * q + 4, first : first + count].rearrange("g r n -> r g n").bitcast(I32),
+                )
+
+        def zero(engine, tile):
+            engine.memset(tile[:].bitcast(I32), 0)
+
+        bw = keep.tile([P, N], BF16, name="bw")
+        ident = keep.tile([P, P], BF16, name="ident")
+        neg = keep.tile([P, P], BF16, name="neg")
+        eps = keep.tile([P, 1], F32, name="eps")
+        cs0 = keep.tile([P, 2, 2, PAIRS], BF16, name="cs0")
+        cs1 = keep.tile([P, 2, TILES - 2, PAIRS], BF16, name="cs1")
+
+        zero(nc.vector, x_planes[0])
+        zero(nc.vector, w_planes[0])
+        nc.gpsimd.memset(bw[:].bitcast(I32), 0)
+        nc.gpsimd.dma_start(out=bw[0:8, :], in_=proj_b.rearrange("(r n) -> r n", r=8))
+        nc.gpsimd.dma_start(out=bw[8:16, :], in_=norm_w.rearrange("(r n) -> r n", r=8))
+        make_identity(nc, ident[:])
+        for i, f in enumerate((freqs_cos, freqs_sin)):
+            nc.gpsimd.dma_start(out=cs0[:, i, :, :], in_=f[0 : 2 * P, :].rearrange("(t p) j -> p t j", p=P))
+        nc.vector.memset(eps[:], EPS)
+        nc.scalar.activation(out=neg[:], in_=ident[:], func=ACT.Copy, scale=-1.0)
+        zero(nc.vector, w_planes[1])
+        for i in (2, 3, 4):
+            zero(nc.gpsimd, w_planes[i])
+        zero(nc.gpsimd, x_planes[1])
+
+        load_codes(x_codes[0], x_words, *x_parts[0], 0, 2)
+        load_codes(w_codes[0], w_words, *SEGMENTS[0], 0, 2)
+        load_scales(x_planes[0], x_scales, *x_parts[0])
+        load_scales(w_planes[0], w_scales, *SEGMENTS[0])
+        load_codes(x_codes[0], x_words, *x_parts[0], 2, 8)
+        load_codes(w_codes[0], w_words, *SEGMENTS[0], 2, 5)
+        load_codes(w_codes[0], w_words, *SEGMENTS[0], 5, 8)
+        load_scales(w_planes[1], w_scales, *SEGMENTS[1])
+        load_codes(w_codes[1], w_words, *SEGMENTS[1], 0, 4)
+        load_codes(w_codes[1], w_words, *SEGMENTS[1], 4, 8)
+        for i in (2, 3, 4):
+            load_scales(w_planes[i], w_scales, *SEGMENTS[i])
+            load_codes(w_codes[i], w_words, *SEGMENTS[i], 0, 4)
+            load_codes(w_codes[i], w_words, *SEGMENTS[i], 4, 8)
+        load_scales(x_planes[1], x_scales, *x_parts[1])
+        load_codes(x_codes[1], x_words, *x_parts[1], 0, 4)
+        load_codes(x_codes[1], x_words, *x_parts[1], 4, 8)
+        for i, f in enumerate((freqs_cos, freqs_sin)):
+            nc.sync.dma_start(out=cs1[:, i, :, :], in_=f[2 * P :, :].rearrange("(t p) j -> p t j", p=P))
+
+        b_sb, w_sb = {}, {}
+
+        def spread(dst, row):
+            nc.tensor.matmul(dst, lhsT=ident[:, row : row + 1].to_broadcast([P, P]), rhs=bw[:], start=True, stop=True)
+
+        def prep(c):
+            b_sb[c] = keep.tile([P, CHUNK], BF16, name=f"b{c}")
+            for half in range(2):
+                bank = psum.tile([P, N], F32, name="mx", tag="mx", bufs=4)
+                spread(bank[:], 2 * c + half)
+                nc.scalar.copy(out=b_sb[c][:, half * N : (half + 1) * N], in_=bank[:])
+            if c in V_CHUNKS:
+                w_sb[c] = psum.tile([P, CHUNK], BF16, name=f"wp{c}", bufs=1)
+                for half in range(2):
+                    spread(w_sb[c][:, half * N : (half + 1) * N], 8 + 2 * c + half)
+            else:
+                w_sb[c] = keep.tile([P, CHUNK], F32, name=f"w{c}")
+                for half in range(2):
+                    bank = psum.tile([P, N], F32, name="mx", tag="mx", bufs=4)
+                    spread(bank[:], 8 + 2 * c + half)
+                    nc.scalar.copy(out=w_sb[c][:, half * N : (half + 1) * N], in_=bank[:])
+
+        tabs = {}
+
+        def table(t):
+            tab = psum.tile([P, PAIRS, 3], F32, name="tab", tag="tab", bufs=2)
+            cs, i = (cs0, t) if t < 2 else (cs1, t - 2)
+            for slot, (m, which) in enumerate(((neg, 1), (ident, 0), (ident, 1))):
+                nc.tensor.matmul(tab[:, :, slot], lhsT=m[:], rhs=cs[:, which, i, :], start=True, stop=True)
+            tabs[t] = tab
+
+        def w_slices(k, block):
+            for i, (first, count) in enumerate(SEGMENTS):
+                if first <= block * N < first + count:
+                    at = block * N - first
+                    return w_codes[i][:, k, 2 * at : 2 * (at + N)].bitcast(FP4X4), w_planes[i][:, k, at : at + N]
+
+        def mx(t, block):
+            acc = psum.tile([P, N], F32, name="mx", tag="mx", bufs=4)
+            part, at = (0, t * P) if t < 2 else (1, (t - 2) * P)
+            for k in range(PASSES):
+                codes, plane = w_slices(k, block)
+                nc.tensor.matmul_mx(
+                    out=acc[:],
+                    lhsT=x_codes[part][:, k, 2 * at : 2 * (at + P)].bitcast(FP4X4),
+                    lhsT_scale=x_planes[part][:, k, at : at + P],
+                    rhs=codes,
+                    rhs_scale=plane,
+                    start=(k == 0),
+                    stop=(k == PASSES - 1),
+                )
+            return acc
+
+        groups = [[0, 1]] + [[t] for t in range(2, TILES)]
+        steps = [(t, c) for g in groups for c in range(CHUNKS) for t in g]
+        out_rows = out.rearrange("s f h d -> f s (h d)")
+        squares, rstds, rot, pend = {}, {}, {}, []
+
+        def finish(t, c):
+            r = rot.pop((t, c))
+            nc.scalar.activation(out=r[:], in_=r[:], func=ACT.Copy, scale=rstds[t][:])
+            for half in range(2):
+                nc.sync.dma_start(
+                    out=out_rows[2 * t + half, :, c * CHUNK : (c + 1) * CHUNK],
+                    in_=r[64 * half : 64 * (half + 1), :],
+                )
+
+        def rotate_a(t, g):
+            r = work.tile([P, CHUNK], F32, name="r", bufs=10)
+            gv = g[:].rearrange("p (h j e) -> p h j e", h=HPC, e=2)
+            nc.vector.tensor_tensor(
+                out=r[:].rearrange("p (h j e) -> p h j e", h=HPC, e=2),
+                in0=gv[:, :, :, 0:1].to_broadcast([P, HPC, PAIRS, 2]),
+                in1=tabs[t][:, :, 1:3].unsqueeze(1).to_broadcast([P, HPC, PAIRS, 2]),
+                op=ALU.mult,
+            )
+            return r
+
+        def rotate_b(t, g):
+            s = work.tile([P, CHUNK], F32, name="s", bufs=2)
+            gv = g[:].rearrange("p (h j e) -> p h j e", h=HPC, e=2)
+            nc.vector.tensor_tensor(
+                out=s[:].rearrange("p (h j e) -> p h j e", h=HPC, e=2),
+                in0=gv[:, :, :, 1:2].to_broadcast([P, HPC, PAIRS, 2]),
+                in1=tabs[t][:, :, 0:2].unsqueeze(1).to_broadcast([P, HPC, PAIRS, 2]),
+                op=ALU.mult,
+            )
+            return s
+
+        prep(0)
+        table(0)
+        table(1)
+        prep(1)
+        accs = {}
+        prev = None
+        for n in range(len(steps) + 1):
+            cur = None
+            if n < len(steps):
+                t, c = steps[n]
+                if t == 0 and c in (1, 2):
+                    prep(c + 1)
+                if t >= 2 and c == 0:
+                    table(t)
+                if (t, c) == (0, 0):
+                    for block in range(2):
+                        for tt in range(2):
+                            accs[tt, block] = mx(tt, block)
+                elif (t, c) != (1, 0):
+                    for block in (2 * c, 2 * c + 1):
+                        accs[t, block] = mx(t, block)
+                h = work.tile([P, CHUNK], F32, name="h", bufs=3)
+                for half in range(2):
+                    cols = slice(half * N, (half + 1) * N)
+                    nc.vector.tensor_tensor(out=h[:, cols], in0=accs.pop((t, 2 * c + half))[:], in1=b_sb[c][:, cols], op=ALU.add)
+                if c == 0:
+                    squares[t] = work.tile([P, CHUNKS], F32, name="ss", bufs=4)
+                junk = work.tile([P, CHUNK], BF16, name="junk", bufs=2)
+                nc.scalar.activation(out=junk[:], in_=h[:], func=ACT.Square, accum_out=squares[t][:, c : c + 1])
+                g = work.tile([P, CHUNK], F32, name="g", bufs=3)
+                cur = (t, c, g)
+            if prev:
+                r = rotate_a(prev[0], prev[2])
+            if cur:
+                engine = nc.vector if c in V_CHUNKS else nc.gpsimd
+                engine.tensor_tensor(out=g[:], in0=h[:], in1=w_sb[c][:], op=ALU.mult)
+            if prev:
+                s = rotate_b(prev[0], prev[2])
+                nc.gpsimd.tensor_tensor(out=r[:], in0=r[:], in1=s[:], op=ALU.add)
+                rot[prev[0], prev[1]] = r
+            count = (2 if pend and pend[0][0] < 2 else 1) if cur else len(pend)
+            for i in range(min(count, len(pend))):
+                finish(*pend.pop(0))
+            if cur and c == CHUNKS - 1:
+                total = work.tile([P, 1], F32, name="total", bufs=4)
+                scrap = work.tile([P, CHUNKS], F32, name="scrap", bufs=4)
+                rstd = work.tile([P, 1], F32, name="rstd", bufs=4)
+                nc.scalar.activation(out=scrap[:], in_=squares[t][:], func=ACT.Copy, accum_out=total[:])
+                nc.scalar.activation(out=rstd[:], in_=total[:], func=ACT.Abs_reciprocal_sqrt, scale=1.0 / D, bias=eps[:])
+                rstds[t] = rstd
+                pend.extend((t, cc) for cc in range(CHUNKS))
+            prev = cur
+        for item in list(pend):
+            finish(*item)

@@ -29,6 +29,9 @@ FLOPS = 2 * ROWS * D * D
 
 SEGMENTS = [(0, 512), (512, 512), (1024, 1024), (2048, 1024), (3072, 1024)]
 V_CHUNKS = (1, 3)
+TAIL = [("s", 0, 0, 0, 512), ("s", 0, 0, 512, 512), ("s", 1, 0, 0, 512), ("s", 1, 0, 512, 512), ("s", 2, 0, 0, 512), ("v", 2, 0, 512, 512), ("v", 3, 0, 0, 512), ("v", 3, 512, 0, 512)]
+LAG2 = 3
+LAST = [(0, 0, 1024, "g", "g"), (1, 0, 1024, "v", "g"), (2, 0, 1024, "g", "g"), (3, 0, 512, "v", "g"), (3, 512, 512, "v", "v")]
 
 
 def tile_temporalattention_pa_kernel(
@@ -66,31 +69,32 @@ def tile_temporalattention_pa_kernel(
         bw = keep.tile([P, N], BF16, name="bw")
         ident = keep.tile([P, P], BF16, name="ident")
         neg = keep.tile([P, P], BF16, name="neg")
-        eps = keep.tile([P, 1], F32, name="eps")
+        eps = keep.tile([P, 2], F32, name="eps")
         cs0 = keep.tile([P, 2, 2, PAIRS], BF16, name="cs0")
         cs1 = keep.tile([P, 2, TILES - 2, PAIRS], BF16, name="cs1")
 
+        zero(nc.vector, bw)
         zero(nc.vector, x_planes[0])
         zero(nc.vector, w_planes[0])
-        nc.gpsimd.memset(bw[:].bitcast(I32), 0)
-        nc.gpsimd.dma_start(out=bw[0:8, :], in_=proj_b.rearrange("(r n) -> r n", r=8))
-        nc.gpsimd.dma_start(out=bw[8:16, :], in_=norm_w.rearrange("(r n) -> r n", r=8))
         make_identity(nc, ident[:])
+        nc.scalar.dma_start(out=bw[0:8, :], in_=proj_b.rearrange("(r n) -> r n", r=8))
+        nc.scalar.dma_start(out=bw[8:16, :], in_=norm_w.rearrange("(r n) -> r n", r=8))
         for i, f in enumerate((freqs_cos, freqs_sin)):
             nc.gpsimd.dma_start(out=cs0[:, i, :, :], in_=f[0 : 2 * P, :].rearrange("(t p) j -> p t j", p=P))
-        nc.vector.memset(eps[:], EPS)
+        nc.vector.memset(eps[:, 0:1], EPS / (CHUNKS - 1))
+        nc.vector.memset(eps[:, 1:2], EPS / (len(LAST) - 1))
         nc.scalar.activation(out=neg[:], in_=ident[:], func=ACT.Copy, scale=-1.0)
         zero(nc.vector, w_planes[1])
         for i in (2, 3, 4):
             zero(nc.gpsimd, w_planes[i])
         zero(nc.gpsimd, x_planes[1])
 
-        load_codes(x_codes[0], x_words, *x_parts[0], 0, 2)
-        load_codes(w_codes[0], w_words, *SEGMENTS[0], 0, 2)
+        load_codes(x_codes[0], x_words, *x_parts[0], 0, 3)
+        load_codes(w_codes[0], w_words, *SEGMENTS[0], 0, 3)
         load_scales(x_planes[0], x_scales, *x_parts[0])
         load_scales(w_planes[0], w_scales, *SEGMENTS[0])
-        load_codes(x_codes[0], x_words, *x_parts[0], 2, 8)
-        load_codes(w_codes[0], w_words, *SEGMENTS[0], 2, 5)
+        load_codes(x_codes[0], x_words, *x_parts[0], 3, 8)
+        load_codes(w_codes[0], w_words, *SEGMENTS[0], 3, 5)
         load_codes(w_codes[0], w_words, *SEGMENTS[0], 5, 8)
         load_scales(w_planes[1], w_scales, *SEGMENTS[1])
         load_codes(w_codes[1], w_words, *SEGMENTS[1], 0, 4)
@@ -110,22 +114,25 @@ def tile_temporalattention_pa_kernel(
         def spread(dst, row):
             nc.tensor.matmul(dst, lhsT=ident[:, row : row + 1].to_broadcast([P, P]), rhs=bw[:], start=True, stop=True)
 
-        def prep(c):
+        for c in range(CHUNKS):
             b_sb[c] = keep.tile([P, CHUNK], BF16, name=f"b{c}")
-            for half in range(2):
-                bank = psum.tile([P, N], F32, name="mx", tag="mx", bufs=4)
-                spread(bank[:], 2 * c + half)
-                nc.scalar.copy(out=b_sb[c][:, half * N : (half + 1) * N], in_=bank[:])
-            if c in V_CHUNKS:
-                w_sb[c] = psum.tile([P, CHUNK], BF16, name=f"wp{c}", bufs=1)
-                for half in range(2):
-                    spread(w_sb[c][:, half * N : (half + 1) * N], 8 + 2 * c + half)
-            else:
+            if c not in V_CHUNKS:
                 w_sb[c] = keep.tile([P, CHUNK], F32, name=f"w{c}")
-                for half in range(2):
-                    bank = psum.tile([P, N], F32, name="mx", tag="mx", bufs=4)
-                    spread(bank[:], 8 + 2 * c + half)
-                    nc.scalar.copy(out=w_sb[c][:, half * N : (half + 1) * N], in_=bank[:])
+
+        def spread_b(c, half, tag, bufs, copy):
+            bank = psum.tile([P, N], F32, name="bank", tag=tag, bufs=bufs)
+            spread(bank[:], 2 * c + half)
+            copy(out=b_sb[c][:, half * N : (half + 1) * N], in_=bank[:])
+
+        def spread_w(c, half, tag, bufs, copy):
+            if c in V_CHUNKS:
+                if half == 0:
+                    w_sb[c] = psum.tile([P, CHUNK], BF16, name=f"wp{c}", tag=f"wp{c}", bufs=1)
+                spread(w_sb[c][:, half * N : (half + 1) * N], 8 + 2 * c + half)
+            else:
+                bank = psum.tile([P, N], F32, name="bank", tag=tag, bufs=bufs)
+                spread(bank[:], 8 + 2 * c + half)
+                copy(out=w_sb[c][:, half * N : (half + 1) * N], in_=bank[:])
 
         tabs = {}
 
@@ -142,109 +149,152 @@ def tile_temporalattention_pa_kernel(
                     at = block * N - first
                     return w_codes[i][:, k, 2 * at : 2 * (at + N)].bitcast(FP4X4), w_planes[i][:, k, at : at + N]
 
-        def mx(t, block):
-            acc = psum.tile([P, N], F32, name="mx", tag="mx", bufs=4)
-            part, at = (0, t * P) if t < 2 else (1, (t - 2) * P)
+        def mx(rows, block):
+            banks = {t: psum.tile([P, N], F32, name="mx", tag="mx", bufs=4) for t in rows}
             for k in range(PASSES):
                 codes, plane = w_slices(k, block)
-                nc.tensor.matmul_mx(
-                    out=acc[:],
-                    lhsT=x_codes[part][:, k, 2 * at : 2 * (at + P)].bitcast(FP4X4),
-                    lhsT_scale=x_planes[part][:, k, at : at + P],
-                    rhs=codes,
-                    rhs_scale=plane,
-                    start=(k == 0),
-                    stop=(k == PASSES - 1),
-                )
-            return acc
+                for t in rows:
+                    part, at = (0, t * P) if t < 2 else (1, (t - 2) * P)
+                    nc.tensor.matmul_mx(
+                        out=banks[t][:],
+                        lhsT=x_codes[part][:, k, 2 * at : 2 * (at + P)].bitcast(FP4X4),
+                        lhsT_scale=x_planes[part][:, k, at : at + P],
+                        rhs=codes,
+                        rhs_scale=plane,
+                        start=(k == 0),
+                        stop=(k == PASSES - 1),
+                    )
+            for t in rows:
+                accs[t, block] = banks[t]
 
-        groups = [[0, 1]] + [[t] for t in range(2, TILES)]
-        steps = [(t, c) for g in groups for c in range(CHUNKS) for t in g]
+        full = lambda c: (c, 0, CHUNK, "v" if c in V_CHUNKS else "g", "g")
+        steps = [(t,) + full(c) for c in range(CHUNKS) for t in (0, 1)]
+        steps += [(t,) + full(c) for t in range(2, TILES - 1) for c in range(CHUNKS)]
+        steps += [(TILES - 1,) + unit for unit in LAST]
         out_rows = out.rearrange("s f h d -> f s (h d)")
-        squares, rstds, rot, pend = {}, {}, {}, []
+        accs, squares, rstds, rot, pend = {}, {}, {}, {}, []
 
-        def finish(t, c):
-            r = rot.pop((t, c))
+        def store(queue, t, half, r, first, a, n):
+            queue.dma_start(
+                out=out_rows[2 * t + half, :, first + a : first + a + n],
+                in_=r[64 * half : 64 * (half + 1), a : a + n],
+            )
+
+        def finish(t, c, a, n):
+            r = rot.pop((t, c, a))
             nc.scalar.activation(out=r[:], in_=r[:], func=ACT.Copy, scale=rstds[t][:])
             for half in range(2):
-                nc.sync.dma_start(
-                    out=out_rows[2 * t + half, :, c * CHUNK : (c + 1) * CHUNK],
-                    in_=r[64 * half : 64 * (half + 1), :],
-                )
+                store(nc.sync, t, half, r, c * CHUNK + a, 0, n)
 
-        def rotate_a(t, g):
-            r = work.tile([P, CHUNK], F32, name="r", bufs=10)
-            gv = g[:].rearrange("p (h j e) -> p h j e", h=HPC, e=2)
+        def rotate(t, g, n, which):
+            heads = n // HEAD
+            tag, bufs = ("r", 10) if which == 0 else ("s", 2)
+            r = work.tile([P, n], F32, name="prod", tag=tag, bufs=bufs)
+            gv = g[:].rearrange("p (h j e) -> p h j e", h=heads, e=2)
             nc.vector.tensor_tensor(
-                out=r[:].rearrange("p (h j e) -> p h j e", h=HPC, e=2),
-                in0=gv[:, :, :, 0:1].to_broadcast([P, HPC, PAIRS, 2]),
-                in1=tabs[t][:, :, 1:3].unsqueeze(1).to_broadcast([P, HPC, PAIRS, 2]),
+                out=r[:].rearrange("p (h j e) -> p h j e", h=heads, e=2),
+                in0=gv[:, :, :, which : which + 1].to_broadcast([P, heads, PAIRS, 2]),
+                in1=tabs[t][:, :, 1 - which : 3 - which].unsqueeze(1).to_broadcast([P, heads, PAIRS, 2]),
                 op=ALU.mult,
             )
             return r
 
-        def rotate_b(t, g):
-            s = work.tile([P, CHUNK], F32, name="s", bufs=2)
-            gv = g[:].rearrange("p (h j e) -> p h j e", h=HPC, e=2)
-            nc.vector.tensor_tensor(
-                out=s[:].rearrange("p (h j e) -> p h j e", h=HPC, e=2),
-                in0=gv[:, :, :, 1:2].to_broadcast([P, HPC, PAIRS, 2]),
-                in1=tabs[t][:, :, 0:2].unsqueeze(1).to_broadcast([P, HPC, PAIRS, 2]),
-                op=ALU.mult,
-            )
-            return s
+        spread_b(0, 0, "wp1", 1, nc.vector.tensor_copy)
+        spread_b(0, 1, "wp3", 1, nc.vector.tensor_copy)
+        spread_w(0, 0, "mx", 4, nc.scalar.copy)
+        spread_w(0, 1, "mx", 4, nc.scalar.copy)
+        spread_b(1, 0, "wp3", 1, nc.vector.tensor_copy)
+        spread_b(1, 1, "wp1", 1, nc.vector.tensor_copy)
+        jobs = [(table, 0), (table, 1)]
+        for c in range(1, CHUNKS):
+            for f in (spread_b, spread_w)[1 if c == 1 else 0 :]:
+                jobs += [(f, c, half, "wp3", 1, nc.scalar.copy) for half in range(2)]
 
-        prep(0)
-        table(0)
-        table(1)
-        prep(1)
-        accs = {}
-        prev = None
-        for n in range(len(steps) + 1):
+        def job():
+            if jobs:
+                f, *args = jobs.pop(0)
+                f(*args)
+
+        waiting = []
+        done_units = {}
+        for step in steps + [None] * 3:
             cur = None
-            if n < len(steps):
-                t, c = steps[n]
-                if t == 0 and c in (1, 2):
-                    prep(c + 1)
-                if t >= 2 and c == 0:
+            if step:
+                t, c, a, n, gain, add = step
+                first = (t, len([1 for s in steps if s[0] == t]))
+                index = done_units.get(t, 0)
+                done_units[t] = index + 1
+                count = first[1]
+                if t >= 2 and index == 1:
                     table(t)
+                blocks = [(c * CHUNK + a) // N + i for i in range(n // N)]
                 if (t, c) == (0, 0):
-                    for block in range(2):
-                        for tt in range(2):
-                            accs[tt, block] = mx(tt, block)
+                    for block in blocks:
+                        mx((0, 1), block)
+                        for i in range(3):
+                            job()
                 elif (t, c) != (1, 0):
-                    for block in (2 * c, 2 * c + 1):
-                        accs[t, block] = mx(t, block)
-                h = work.tile([P, CHUNK], F32, name="h", bufs=3)
-                for half in range(2):
-                    cols = slice(half * N, (half + 1) * N)
-                    nc.vector.tensor_tensor(out=h[:, cols], in0=accs.pop((t, 2 * c + half))[:], in1=b_sb[c][:, cols], op=ALU.add)
-                if c == 0:
-                    squares[t] = work.tile([P, CHUNKS], F32, name="ss", bufs=4)
-                junk = work.tile([P, CHUNK], BF16, name="junk", bufs=2)
-                nc.scalar.activation(out=junk[:], in_=h[:], func=ACT.Square, accum_out=squares[t][:, c : c + 1])
-                g = work.tile([P, CHUNK], F32, name="g", bufs=3)
-                cur = (t, c, g)
-            if prev:
-                r = rotate_a(prev[0], prev[2])
+                    for block in blocks:
+                        mx((t,), block)
+                        job()
+                h = work.tile([P, n], F32, name="h", tag="h", bufs=3)
+                for i, block in enumerate(blocks):
+                    cols = slice(i * N, (i + 1) * N)
+                    nc.vector.tensor_tensor(out=h[:, cols], in0=accs.pop((t, block))[:], in1=b_sb[c][:, a + i * N : a + (i + 1) * N], op=ALU.add)
+                if index == 0:
+                    squares[t] = work.tile([P, 8], F32, name="ss", tag="ss", bufs=4)
+                junk = work.tile([P, n], BF16, name="junk", tag="junk", bufs=2)
+                nc.scalar.activation(out=junk[:], in_=h[:], func=ACT.Square, accum_out=squares[t][:, index : index + 1])
+                g = work.tile([P, n], F32, name="g", tag="g", bufs=3)
+                cur = (t, c, a, n, g, add)
+            lag = max(len(waiting) - 1, 0) if cur is None else 2 if t == TILES - 1 and index >= LAG2 else 1
+            old = []
+            while len(waiting) + (1 if cur else 0) > lag and waiting:
+                old.append(waiting.pop(0))
+            prods = []
+            for u in old:
+                prods.append(rotate(u[0], u[4], u[3], 0))
+                if cur:
+                    break
             if cur:
-                engine = nc.vector if c in V_CHUNKS else nc.gpsimd
-                engine.tensor_tensor(out=g[:], in0=h[:], in1=w_sb[c][:], op=ALU.mult)
-            if prev:
-                s = rotate_b(prev[0], prev[2])
-                nc.gpsimd.tensor_tensor(out=r[:], in0=r[:], in1=s[:], op=ALU.add)
-                rot[prev[0], prev[1]] = r
-            count = (2 if pend and pend[0][0] < 2 else 1) if cur else len(pend)
-            for i in range(min(count, len(pend))):
-                finish(*pend.pop(0))
-            if cur and c == CHUNKS - 1:
-                total = work.tile([P, 1], F32, name="total", bufs=4)
-                scrap = work.tile([P, CHUNKS], F32, name="scrap", bufs=4)
-                rstd = work.tile([P, 1], F32, name="rstd", bufs=4)
-                nc.scalar.activation(out=scrap[:], in_=squares[t][:], func=ACT.Copy, accum_out=total[:])
-                nc.scalar.activation(out=rstd[:], in_=total[:], func=ACT.Abs_reciprocal_sqrt, scale=1.0 / D, bias=eps[:])
-                rstds[t] = rstd
-                pend.extend((t, cc) for cc in range(CHUNKS))
-            prev = cur
-        for item in list(pend):
-            finish(*item)
+                engine = nc.vector if gain == "v" else nc.gpsimd
+                engine.tensor_tensor(out=g[:], in0=h[:], in1=w_sb[c][:, a : a + n], op=ALU.mult)
+                waiting.append(cur)
+            for i, u in enumerate(old):
+                r = prods[i]
+                s = rotate(u[0], u[4], u[3], 1)
+                engine = nc.vector if u[5] == "v" else nc.gpsimd
+                engine.tensor_tensor(out=r[:], in0=r[:], in1=s[:], op=ALU.add)
+                rot[u[0], u[1], u[2]] = r
+            if cur:
+                for i in range(min(len(pend), 2 if pend and pend[0][0] < 2 else 1)):
+                    finish(*pend.pop(0))
+                if index == count - 2:
+                    base = work.tile([P, 1], F32, name="base", tag="base", bufs=4)
+                    scrap = work.tile([P, 8], F32, name="scrap", tag="scrap", bufs=4)
+                    which = 1 if t == TILES - 1 else 0
+                    nc.scalar.activation(out=scrap[:, 0 : index + 1], in_=squares[t][:, 0 : index + 1], func=ACT.Identity, scale=1.0 / D, bias=eps[:, which : which + 1], accum_out=base[:])
+                    rstds[t] = base
+                if index == count - 1:
+                    rstd = work.tile([P, 1], F32, name="rstd", tag="rstd", bufs=4)
+                    nc.scalar.activation(out=rstd[:], in_=squares[t][:, index : index + 1], func=ACT.Abs_reciprocal_sqrt, scale=1.0 / D, bias=rstds[t][:])
+                    rstds[t] = rstd
+                    if t < TILES - 1:
+                        pend.extend(s[:4] for s in steps if s[0] == t)
+
+        t = TILES - 1
+
+        def scale(engine, r, a, n):
+            v = r[:, a : a + n]
+            if engine == "s":
+                nc.scalar.activation(out=v, in_=v, func=ACT.Copy, scale=rstds[t][:])
+            elif engine == "v":
+                nc.vector.tensor_scalar(out=v, in0=v, scalar1=rstds[t][:], scalar2=None, op0=ALU.mult)
+            else:
+                nc.gpsimd.tensor_scalar(out=v, in0=v, scalar1=rstds[t][:], scalar2=0.0, op0=ALU.mult, op1=ALU.add)
+
+        for engine, c, unit, a, n in TAIL:
+            r = rot[t, c, unit]
+            scale(engine, r, a, n)
+            store(nc.sync, t, 0, r, c * CHUNK + unit, a, n)
+            store(nc.scalar if engine == "s" else nc.sync, t, 1, r, c * CHUNK + unit, a, n)

@@ -29,9 +29,9 @@ FLOPS = 2 * ROWS * D * D
 
 SEGMENTS = [(0, 512), (512, 512), (1024, 1024), (2048, 1024), (3072, 1024)]
 V_CHUNKS = (1, 3)
-TAIL = [("s", 0, 0, 0, 512), ("s", 0, 0, 512, 512), ("s", 1, 0, 0, 512), ("s", 1, 0, 512, 512), ("s", 2, 0, 0, 512), ("v", 2, 0, 512, 512), ("v", 3, 0, 0, 512), ("v", 3, 512, 0, 512)]
-LAG2 = 3
-LAST = [(0, 0, 1024, "g", "g"), (1, 0, 1024, "v", "g"), (2, 0, 1024, "g", "g"), (3, 0, 512, "v", "g"), (3, 512, 512, "v", "v")]
+TAIL = [("s", 0, 0, 512), ("s", 0, 512, 512), ("s", 1, 0, 512), ("s", 1, 512, 512), ("s", 2, 0, 512), ("v", 2, 512, 512), ("v", 3, 0, 512), ("v", 4, 0, 512)]
+LAST = [(0, 0, 1024), (1, 0, 1024), (2, 0, 1024), (3, 0, 512), (3, 512, 512)]
+PLAN = [("b", 0, ""), ("q", 0, ""), ("r", -1, ""), ("w", 0, "g"), ("s", -1, ""), ("j", -1, "g"), ("f", 99, ""), ("b", 1, ""), ("q", 1, ""), ("r", 0, ""), ("w", 1, "v"), ("s", 0, ""), ("j", 0, "g"), ("f", 99, ""), ("b", 2, ""), ("q", 2, ""), ("r", 1, ""), ("w", 2, "g"), ("s", 1, ""), ("j", 1, "g"), ("f", 99, ""), ("b", 3, ""), ("q", 3, ""), ("w", 3, "v"), ("f", 99, ""), ("b", 4, ""), ("q", 4, ""), ("r", 2, ""), ("w", 4, "v"), ("s", 2, ""), ("j", 2, "g"), ("r", 3, ""), ("s", 3, ""), ("j", 3, "g"), ("r", 4, ""), ("s", 4, ""), ("j", 4, "v")]
 
 
 def tile_temporalattention_pa_kernel(
@@ -57,10 +57,10 @@ def tile_temporalattention_pa_kernel(
             )
 
         def load_scales(tile, scales, first, count):
-            for q in range(4):
+            for r in range(4):
                 nc.sync.dma_start(
-                    out=tile[32 * q : 32 * q + 4, :, :].bitcast(I32),
-                    in_=scales[:, 4 * q : 4 * q + 4, first : first + count].rearrange("g r n -> r g n").bitcast(I32),
+                    out=tile[r:P:32, :, :].bitcast(I32),
+                    in_=scales[:, r:16:4, first : first + count].rearrange("g r n -> r g n").bitcast(I32),
                 )
 
         def zero(engine, tile):
@@ -167,37 +167,78 @@ def tile_temporalattention_pa_kernel(
             for t in rows:
                 accs[t, block] = banks[t]
 
-        full = lambda c: (c, 0, CHUNK, "v" if c in V_CHUNKS else "g", "g")
-        steps = [(t,) + full(c) for c in range(CHUNKS) for t in (0, 1)]
-        steps += [(t,) + full(c) for t in range(2, TILES - 1) for c in range(CHUNKS)]
-        steps += [(TILES - 1,) + unit for unit in LAST]
         out_rows = out.rearrange("s f h d -> f s (h d)")
-        accs, squares, rstds, rot, pend = {}, {}, {}, {}, []
+        accs, squares, rstds, parts, pend = {}, {}, {}, {}, []
 
-        def store(queue, t, half, r, first, a, n):
-            queue.dma_start(
-                out=out_rows[2 * t + half, :, first + a : first + a + n],
-                in_=r[64 * half : 64 * (half + 1), a : a + n],
-            )
+        def add_bias(u):
+            t, c, a, n = u
+            h = work.tile([P, n], F32, name="h", tag="h", bufs=3)
+            for i in range(0, n, N):
+                bank = accs.pop((t, (c * CHUNK + a + i) // N))
+                nc.vector.tensor_tensor(out=h[:, i : i + N], in0=bank[:], in1=b_sb[c][:, a + i : a + i + N], op=ALU.add)
+            parts[u] = {"h": h}
 
-        def finish(t, c, a, n):
-            r = rot.pop((t, c, a))
-            nc.scalar.activation(out=r[:], in_=r[:], func=ACT.Copy, scale=rstds[t][:])
-            for half in range(2):
-                store(nc.sync, t, half, r, c * CHUNK + a, 0, n)
+        def square(u, index, count):
+            t, n = u[0], u[3]
+            if index == 0:
+                squares[t] = work.tile([P, 8], F32, name="ss", tag="ss", bufs=4)
+            junk = work.tile([P, n], BF16, name="junk", tag="junk", bufs=2)
+            nc.scalar.activation(out=junk[:], in_=parts[u]["h"][:], func=ACT.Square, accum_out=squares[t][:, index : index + 1])
+            if index == count - 2:
+                base = work.tile([P, 1], F32, name="base", tag="base", bufs=4)
+                scrap = work.tile([P, 8], F32, name="scrap", tag="scrap", bufs=4)
+                which = 1 if t == TILES - 1 else 0
+                nc.scalar.activation(out=scrap[:, 0 : index + 1], in_=squares[t][:, 0 : index + 1], func=ACT.Identity, scale=1.0 / D, bias=eps[:, which : which + 1], accum_out=base[:])
+                rstds[t] = base
+            if index == count - 1:
+                rstd = work.tile([P, 1], F32, name="rstd", tag="rstd", bufs=4)
+                nc.scalar.activation(out=rstd[:], in_=squares[t][:, index : index + 1], func=ACT.Abs_reciprocal_sqrt, scale=1.0 / D, bias=rstds[t][:])
+                rstds[t] = rstd
 
-        def rotate(t, g, n, which):
+        def gain(u, engine):
+            t, c, a, n = u
+            g = work.tile([P, n], F32, name="g", tag="g", bufs=3)
+            engine.tensor_tensor(out=g[:], in0=parts[u]["h"][:], in1=w_sb[c][:, a : a + n], op=ALU.mult)
+            parts[u]["g"] = g
+
+        def turn(u, which):
+            t, c, a, n = u
             heads = n // HEAD
-            tag, bufs = ("r", 10) if which == 0 else ("s", 2)
-            r = work.tile([P, n], F32, name="prod", tag=tag, bufs=bufs)
-            gv = g[:].rearrange("p (h j e) -> p h j e", h=heads, e=2)
+            tag, bufs = (("r", 10), ("s", 2))[which]
+            prod = work.tile([P, n], F32, name="prod", tag=tag, bufs=bufs)
             nc.vector.tensor_tensor(
-                out=r[:].rearrange("p (h j e) -> p h j e", h=heads, e=2),
-                in0=gv[:, :, :, which : which + 1].to_broadcast([P, heads, PAIRS, 2]),
+                out=prod[:].rearrange("p (h j e) -> p h j e", h=heads, e=2),
+                in0=parts[u]["g"][:].rearrange("p (h j e) -> p h j e", h=heads, e=2)[:, :, :, which : which + 1].to_broadcast([P, heads, PAIRS, 2]),
                 in1=tabs[t][:, :, 1 - which : 3 - which].unsqueeze(1).to_broadcast([P, heads, PAIRS, 2]),
                 op=ALU.mult,
             )
-            return r
+            parts[u][tag] = prod
+
+        def join(u, engine):
+            r, s = parts[u]["r"], parts[u]["s"]
+            engine.tensor_tensor(out=r[:], in0=r[:], in1=s[:], op=ALU.add)
+
+        def scale(u, a, n, engine):
+            v = parts[u]["r"][:, a : a + n]
+            rstd = rstds[u[0]]
+            if engine == "s":
+                nc.scalar.activation(out=v, in_=v, func=ACT.Copy, scale=rstd[:])
+            elif engine == "v":
+                nc.vector.tensor_scalar(out=v, in0=v, scalar1=rstd[:], scalar2=None, op0=ALU.mult)
+            else:
+                nc.gpsimd.tensor_scalar(out=v, in0=v, scalar1=rstd[:], scalar2=0.0, op0=ALU.mult, op1=ALU.add)
+
+        def store(u, a, n, queues):
+            t, c, first = u[:3]
+            for half in range(2):
+                queues[half].dma_start(
+                    out=out_rows[2 * t + half, :, c * CHUNK + first + a : c * CHUNK + first + a + n],
+                    in_=parts[u]["r"][64 * half : 64 * (half + 1), a : a + n],
+                )
+
+        def finish(u):
+            scale(u, 0, u[3], "s")
+            store(u, 0, u[3], (nc.sync, nc.sync))
 
         spread_b(0, 0, "wp1", 1, nc.vector.tensor_copy)
         spread_b(0, 1, "wp3", 1, nc.vector.tensor_copy)
@@ -215,86 +256,59 @@ def tile_temporalattention_pa_kernel(
                 f, *args = jobs.pop(0)
                 f(*args)
 
-        waiting = []
-        done_units = {}
-        for step in steps + [None] * 3:
-            cur = None
-            if step:
-                t, c, a, n, gain, add = step
-                first = (t, len([1 for s in steps if s[0] == t]))
-                index = done_units.get(t, 0)
-                done_units[t] = index + 1
-                count = first[1]
-                if t >= 2 and index == 1:
-                    table(t)
-                blocks = [(c * CHUNK + a) // N + i for i in range(n // N)]
+        engines = {"v": nc.vector, "g": nc.gpsimd}
+        steps = [(t, c, 0, CHUNK) for c in range(CHUNKS) for t in (0, 1)]
+        steps += [(t, c, 0, CHUNK) for t in range(2, TILES - 1) for c in range(CHUNKS)]
+        prev = None
+        for u in steps:
+            t, c = u[:2]
+            if t >= 2 and c == 1:
+                table(t)
+            for block in (2 * c, 2 * c + 1):
                 if (t, c) == (0, 0):
-                    for block in blocks:
-                        mx((0, 1), block)
-                        for i in range(3):
-                            job()
-                elif (t, c) != (1, 0):
-                    for block in blocks:
-                        mx((t,), block)
+                    mx((0, 1), block)
+                    for i in range(3):
                         job()
-                h = work.tile([P, n], F32, name="h", tag="h", bufs=3)
-                for i, block in enumerate(blocks):
-                    cols = slice(i * N, (i + 1) * N)
-                    nc.vector.tensor_tensor(out=h[:, cols], in0=accs.pop((t, block))[:], in1=b_sb[c][:, a + i * N : a + (i + 1) * N], op=ALU.add)
-                if index == 0:
-                    squares[t] = work.tile([P, 8], F32, name="ss", tag="ss", bufs=4)
-                junk = work.tile([P, n], BF16, name="junk", tag="junk", bufs=2)
-                nc.scalar.activation(out=junk[:], in_=h[:], func=ACT.Square, accum_out=squares[t][:, index : index + 1])
-                g = work.tile([P, n], F32, name="g", tag="g", bufs=3)
-                cur = (t, c, a, n, g, add)
-            lag = max(len(waiting) - 1, 0) if cur is None else 2 if t == TILES - 1 and index >= LAG2 else 1
-            old = []
-            while len(waiting) + (1 if cur else 0) > lag and waiting:
-                old.append(waiting.pop(0))
-            prods = []
-            for u in old:
-                prods.append(rotate(u[0], u[4], u[3], 0))
-                if cur:
-                    break
-            if cur:
-                engine = nc.vector if gain == "v" else nc.gpsimd
-                engine.tensor_tensor(out=g[:], in0=h[:], in1=w_sb[c][:, a : a + n], op=ALU.mult)
-                waiting.append(cur)
-            for i, u in enumerate(old):
-                r = prods[i]
-                s = rotate(u[0], u[4], u[3], 1)
-                engine = nc.vector if u[5] == "v" else nc.gpsimd
-                engine.tensor_tensor(out=r[:], in0=r[:], in1=s[:], op=ALU.add)
-                rot[u[0], u[1], u[2]] = r
-            if cur:
-                for i in range(min(len(pend), 2 if pend and pend[0][0] < 2 else 1)):
-                    finish(*pend.pop(0))
-                if index == count - 2:
-                    base = work.tile([P, 1], F32, name="base", tag="base", bufs=4)
-                    scrap = work.tile([P, 8], F32, name="scrap", tag="scrap", bufs=4)
-                    which = 1 if t == TILES - 1 else 0
-                    nc.scalar.activation(out=scrap[:, 0 : index + 1], in_=squares[t][:, 0 : index + 1], func=ACT.Identity, scale=1.0 / D, bias=eps[:, which : which + 1], accum_out=base[:])
-                    rstds[t] = base
-                if index == count - 1:
-                    rstd = work.tile([P, 1], F32, name="rstd", tag="rstd", bufs=4)
-                    nc.scalar.activation(out=rstd[:], in_=squares[t][:, index : index + 1], func=ACT.Abs_reciprocal_sqrt, scale=1.0 / D, bias=rstds[t][:])
-                    rstds[t] = rstd
-                    if t < TILES - 1:
-                        pend.extend(s[:4] for s in steps if s[0] == t)
+                elif (t, c) != (1, 0):
+                    mx((t,), block)
+                    job()
+            add_bias(u)
+            square(u, c, CHUNKS)
+            if prev:
+                turn(prev, 0)
+            gain(u, nc.vector if c in V_CHUNKS else nc.gpsimd)
+            if prev:
+                turn(prev, 1)
+                join(prev, nc.gpsimd)
+            for i in range(min(len(pend), 2 if pend and pend[0][0] < 2 else 1)):
+                finish(pend.pop(0))
+            if c == CHUNKS - 1:
+                pend.extend((t, cc, 0, CHUNK) for cc in range(CHUNKS))
+            prev = u
 
         t = TILES - 1
-
-        def scale(engine, r, a, n):
-            v = r[:, a : a + n]
-            if engine == "s":
-                nc.scalar.activation(out=v, in_=v, func=ACT.Copy, scale=rstds[t][:])
-            elif engine == "v":
-                nc.vector.tensor_scalar(out=v, in0=v, scalar1=rstds[t][:], scalar2=None, op0=ALU.mult)
-            else:
-                nc.gpsimd.tensor_scalar(out=v, in0=v, scalar1=rstds[t][:], scalar2=0.0, op0=ALU.mult, op1=ALU.add)
-
-        for engine, c, unit, a, n in TAIL:
-            r = rot[t, c, unit]
-            scale(engine, r, a, n)
-            store(nc.sync, t, 0, r, c * CHUNK + unit, a, n)
-            store(nc.scalar if engine == "s" else nc.sync, t, 1, r, c * CHUNK + unit, a, n)
+        last = [(t,) + unit for unit in LAST]
+        for i, u in enumerate(last):
+            if i == 1:
+                table(t)
+            for block in range((u[1] * CHUNK + u[2]) // N, (u[1] * CHUNK + u[2] + u[3]) // N):
+                mx((t,), block)
+        for what, i, engine in PLAN:
+            u = prev if i < 0 else last[i] if i < len(last) else None
+            if what == "b":
+                add_bias(u)
+            elif what == "q":
+                square(u, i, len(last))
+            elif what == "w":
+                gain(u, engines[engine])
+            elif what == "r":
+                turn(u, 0)
+            elif what == "s":
+                turn(u, 1)
+            elif what == "j":
+                join(u, engines[engine])
+            elif what == "f":
+                finish(pend.pop(0))
+        for engine, i, a, n in TAIL:
+            scale(last[i], a, n, engine)
+            store(last[i], a, n, (nc.sync, nc.scalar))

@@ -23,15 +23,15 @@ TILES = ROWS // P
 N = 512
 CHUNK = 1024
 CHUNKS = D // CHUNK
-HPC = CHUNK // HEAD
 
 FLOPS = 2 * ROWS * D * D
 
-SEGMENTS = [(0, 512), (512, 512), (1024, 1024), (2048, 1024), (3072, 1024)]
 V_CHUNKS = (1, 3)
-TAIL = [("s", 0, 0, 512), ("s", 0, 512, 512), ("s", 1, 0, 512), ("s", 1, 512, 512), ("s", 2, 0, 512), ("v", 2, 512, 512), ("v", 3, 0, 512), ("v", 4, 0, 512)]
-LAST = [(0, 0, 1024), (1, 0, 1024), (2, 0, 1024), (3, 0, 512), (3, 512, 512)]
-PLAN = [("b", 0, ""), ("q", 0, ""), ("r", -1, ""), ("w", 0, "g"), ("s", -1, ""), ("j", -1, "g"), ("f", 99, ""), ("b", 1, ""), ("q", 1, ""), ("r", 0, ""), ("w", 1, "v"), ("s", 0, ""), ("j", 0, "g"), ("f", 99, ""), ("b", 2, ""), ("q", 2, ""), ("r", 1, ""), ("w", 2, "g"), ("s", 1, ""), ("j", 1, "g"), ("f", 99, ""), ("b", 3, ""), ("q", 3, ""), ("w", 3, "v"), ("f", 99, ""), ("b", 4, ""), ("q", 4, ""), ("r", 2, ""), ("w", 4, "v"), ("s", 2, ""), ("j", 2, "g"), ("r", 3, ""), ("s", 3, ""), ("j", 3, "g"), ("r", 4, ""), ("s", 4, ""), ("j", 4, "v")]
+LAST_TILE = TILES - 1
+TILE_FRAMES = [(0, 1), (2, 3), (13, 14), (15, 16), (17, 18), (19, 20), (21, 22), (4, 5), (6, 7), (8, 9), (10, 12), (11, 23)]
+LAST = [(0, 0, 1024), (1, 0, 1024), (2, 0, 512), (2, 512, 512), (3, 0, 512), (3, 512, 512)]
+PLAN = [("b", 0, ""), ("q", 0, ""), ("f", 99, ""), ("r", -1, ""), ("s", -1, ""), ("w", 0, "g"), ("j", -1, "g"), ("b", 1, ""), ("q", 1, ""), ("f", 99, ""), ("r", 0, ""), ("s", 0, ""), ("b", 2, ""), ("w", 1, "v"), ("b", 3, ""), ("q", 2, ""), ("q", 3, ""), ("r", 1, ""), ("s", 1, ""), ("j", 0, "g"), ("w", 2, "g"), ("w", 3, "g"), ("f", 99, ""), ("b", 4, ""), ("j", 1, "g"), ("f", 99, ""), ("r", 2, ""), ("s", 2, ""), ("b", 5, ""), ("q", 4, ""), ("q", 5, ""), ("w", 4, "v"), ("r", 3, ""), ("s", 3, ""), ("j", 2, "g"), ("w", 5, "v"), ("r", 4, ""), ("s", 4, ""), ("j", 3, "g"), ("j", 4, "g"), ("r", 5, ""), ("s", 5, ""), ("j", 5, "v")]
+TAIL = [("s", 0, 0, 512), ("s", 0, 512, 512), ("s", 1, 0, 512), ("s", 1, 512, 512), ("s", 2, 0, 512), ("s", 3, 0, 512), ("v", 4, 0, 512), ("v", 5, 0, 512)]
 
 
 def tile_temporalattention_pa_kernel(
@@ -44,27 +44,32 @@ def tile_temporalattention_pa_kernel(
         psum = ctx.enter_context(tc.psum_pool(name="psum", bufs=1))
         ctx.enter_context(tc.manual_schedule())
 
-        x_parts = [(0, 256), (256, ROWS - 256)]
-        x_codes = [keep.tile([P, PASSES, 2 * n], U8, name=f"xc{i}", align_bytes=64) for i, (a, n) in enumerate(x_parts)]
-        x_planes = [keep.tile([P, PASSES, n], U8, name=f"xs{i}", align_bytes=64) for i, (a, n) in enumerate(x_parts)]
-        w_codes = [keep.tile([P, PASSES, 2 * n], U8, name=f"wc{i}", align_bytes=64) for i, (a, n) in enumerate(SEGMENTS)]
-        w_planes = [keep.tile([P, PASSES, n], U8, name=f"ws{i}", align_bytes=64) for i, (a, n) in enumerate(SEGMENTS)]
+        def operand(name, cols):
+            codes = keep.tile([P, PASSES, 2 * cols], U8, name=name + "_codes", align_bytes=64)
+            plane = keep.tile([P, PASSES, cols], U8, name=name + "_plane", align_bytes=64)
+            return codes, plane
 
-        def load_codes(tile, words, first, count, k0, k1):
+        def load_codes(tile, at, words, first, count, k0, k1):
             nc.sync.dma_start(
-                out=tile[:, k0:k1, :].bitcast(I32),
+                out=tile[:, k0:k1, 2 * at : 2 * (at + count)].bitcast(I32),
                 in_=words[k0:k1, :, 2 * first : 2 * (first + count)].rearrange("g p n -> p g n").bitcast(I32),
             )
 
-        def load_scales(tile, scales, first, count):
+        def load_scales(tile, at, scales, first, count):
             for r in range(4):
                 nc.sync.dma_start(
-                    out=tile[r:P:32, :, :].bitcast(I32),
+                    out=tile[r:P:32, :, at : at + count].bitcast(I32),
                     in_=scales[:, r:16:4, first : first + count].rearrange("g r n -> r g n").bitcast(I32),
                 )
 
         def zero(engine, tile):
             engine.memset(tile[:].bitcast(I32), 0)
+
+        x_first = operand("xa", 4 * TOKENS)
+        x_high = operand("xb", 13 * TOKENS)
+        x_low = operand("xc", 8 * TOKENS)
+        x_last = operand("xd", 2 * TOKENS)
+        w = [operand(f"w{i}", 512) for i in range(D // 512)]
 
         bw = keep.tile([P, N], BF16, name="bw")
         ident = keep.tile([P, P], BF16, name="ident")
@@ -74,8 +79,8 @@ def tile_temporalattention_pa_kernel(
         cs1 = keep.tile([P, 2, TILES - 2, PAIRS], BF16, name="cs1")
 
         zero(nc.vector, bw)
-        zero(nc.vector, x_planes[0])
-        zero(nc.vector, w_planes[0])
+        zero(nc.vector, x_first[1])
+        zero(nc.vector, w[0][1])
         make_identity(nc, ident[:])
         nc.scalar.dma_start(out=bw[0:8, :], in_=proj_b.rearrange("(r n) -> r n", r=8))
         nc.scalar.dma_start(out=bw[8:16, :], in_=norm_w.rearrange("(r n) -> r n", r=8))
@@ -84,40 +89,63 @@ def tile_temporalattention_pa_kernel(
         nc.vector.memset(eps[:, 0:1], EPS / (CHUNKS - 1))
         nc.vector.memset(eps[:, 1:2], EPS / (len(LAST) - 1))
         nc.scalar.activation(out=neg[:], in_=ident[:], func=ACT.Copy, scale=-1.0)
-        zero(nc.vector, w_planes[1])
-        for i in (2, 3, 4):
-            zero(nc.gpsimd, w_planes[i])
-        zero(nc.gpsimd, x_planes[1])
+        for i in range(1, len(w)):
+            zero(nc.gpsimd, w[i][1])
+        zero(nc.gpsimd, x_high[1])
+        zero(nc.gpsimd, x_low[1])
 
-        load_codes(x_codes[0], x_words, *x_parts[0], 0, 3)
-        load_codes(w_codes[0], w_words, *SEGMENTS[0], 0, 3)
-        load_scales(x_planes[0], x_scales, *x_parts[0])
-        load_scales(w_planes[0], w_scales, *SEGMENTS[0])
-        load_codes(x_codes[0], x_words, *x_parts[0], 3, 8)
-        load_codes(w_codes[0], w_words, *SEGMENTS[0], 3, 5)
-        load_codes(w_codes[0], w_words, *SEGMENTS[0], 5, 8)
-        load_scales(w_planes[1], w_scales, *SEGMENTS[1])
-        load_codes(w_codes[1], w_words, *SEGMENTS[1], 0, 4)
-        load_codes(w_codes[1], w_words, *SEGMENTS[1], 4, 8)
-        for i in (2, 3, 4):
-            load_scales(w_planes[i], w_scales, *SEGMENTS[i])
-            load_codes(w_codes[i], w_words, *SEGMENTS[i], 0, 4)
-            load_codes(w_codes[i], w_words, *SEGMENTS[i], 4, 8)
-        load_scales(x_planes[1], x_scales, *x_parts[1])
-        load_codes(x_codes[1], x_words, *x_parts[1], 0, 4)
-        load_codes(x_codes[1], x_words, *x_parts[1], 4, 8)
-        for i, f in enumerate((freqs_cos, freqs_sin)):
-            nc.sync.dma_start(out=cs1[:, i, :, :], in_=f[2 * P :, :].rearrange("(t p) j -> p t j", p=P))
+        kx, kw, kw2 = 3, 3, 5
+        load_codes(x_first[0], 0, x_words, 0, 256, 0, kx)
+        load_codes(w[0][0], 0, w_words, 0, 512, 0, kw)
+        load_scales(x_first[1], 0, x_scales, 0, 256)
+        load_scales(w[0][1], 0, w_scales, 0, 512)
+        load_codes(x_first[0], 0, x_words, 0, 256, kx, PASSES)
+        load_codes(w[0][0], 0, w_words, 0, 512, kw, kw2)
+        load_codes(w[0][0], 0, w_words, 0, 512, kw2, PASSES)
+        for i in range(1, len(w)):
+            load_scales(w[i][1], 0, w_scales, i * 512, 512)
+            load_codes(w[i][0], 0, w_words, i * 512, 512, 0, 4)
+            load_codes(w[i][0], 0, w_words, i * 512, 512, 4, 8)
+        load_scales(x_high[1], 0, x_scales, 11 * TOKENS, 13 * TOKENS)
+        load_codes(x_high[0], 0, x_words, 11 * TOKENS, 13 * TOKENS, 0, 4)
+        load_codes(x_high[0], 0, x_words, 11 * TOKENS, 13 * TOKENS, 4, 8)
+
+        def load_tables(first, count, frame):
+            for i, f in enumerate((freqs_cos, freqs_sin)):
+                rows = f[frame * TOKENS : (frame + 2 * count) * TOKENS, :]
+                nc.sync.dma_start(out=cs1[:, i, first : first + count, :], in_=rows.rearrange("(t p) j -> p t j", p=P))
+
+        def load_half_table(tile, partitions, frame):
+            for i, f in enumerate((freqs_cos, freqs_sin)):
+                nc.sync.dma_start(out=cs1[partitions, i, tile, :], in_=f[frame * TOKENS : (frame + 1) * TOKENS, :])
+
+        load_tables(0, 5, 13)
+        for at, first, count in ((0, 4, 7), (7, 12, 1)):
+            load_scales(x_low[1], at * TOKENS, x_scales, first * TOKENS, count * TOKENS)
+            load_codes(x_low[0], at * TOKENS, x_words, first * TOKENS, count * TOKENS, 0, 8)
+        load_tables(5, 3, 4)
+        load_half_table(8, slice(0, 64), 10)
+        load_half_table(8, slice(64, 128), 12)
+        load_half_table(9, slice(0, 128, 2), 11)
+        load_half_table(9, slice(1, 128, 2), 23)
+
+        def interleave(piece):
+            which, e = divmod(piece, 2)
+            b = 2 if which == 0 else 1
+            frame = 0 if e == 0 else 12
+            nc.vector.tensor_copy(
+                out=x_last[which][:].rearrange("p k (s e b) -> p k e s b", e=2, b=b)[:, :, e, :, :],
+                in_=x_high[which][:, :, b * frame * TOKENS : b * (frame + 1) * TOKENS].rearrange("p k (s b) -> p k s b", b=b),
+            )
 
         b_sb, w_sb = {}, {}
-
-        def spread(dst, row):
-            nc.tensor.matmul(dst, lhsT=ident[:, row : row + 1].to_broadcast([P, P]), rhs=bw[:], start=True, stop=True)
-
         for c in range(CHUNKS):
             b_sb[c] = keep.tile([P, CHUNK], BF16, name=f"b{c}")
             if c not in V_CHUNKS:
-                w_sb[c] = keep.tile([P, CHUNK], F32, name=f"w{c}")
+                w_sb[c] = keep.tile([P, CHUNK], F32, name=f"g{c}")
+
+        def spread(dst, row):
+            nc.tensor.matmul(dst, lhsT=ident[:, row : row + 1].to_broadcast([P, P]), rhs=bw[:], start=True, stop=True)
 
         def spread_b(c, half, tag, bufs, copy):
             bank = psum.tile([P, N], F32, name="bank", tag=tag, bufs=bufs)
@@ -143,40 +171,42 @@ def tile_temporalattention_pa_kernel(
                 nc.tensor.matmul(tab[:, :, slot], lhsT=m[:], rhs=cs[:, which, i, :], start=True, stop=True)
             tabs[t] = tab
 
-        def w_slices(k, block):
-            for i, (first, count) in enumerate(SEGMENTS):
-                if first <= block * N < first + count:
-                    at = block * N - first
-                    return w_codes[i][:, k, 2 * at : 2 * (at + N)].bitcast(FP4X4), w_planes[i][:, k, at : at + N]
+        def x_tile(t):
+            if t < 2:
+                return x_first, t * P
+            if t < 7:
+                return x_high, (TILE_FRAMES[t][0] - 11) * TOKENS
+            if t < LAST_TILE:
+                return x_low, (t - 7) * P
+            return x_last, 0
+
+        accs, squares, rstds, parts, pend = {}, {}, {}, {}, []
 
         def mx(rows, block):
             banks = {t: psum.tile([P, N], F32, name="mx", tag="mx", bufs=4) for t in rows}
+            seg, at = divmod(block * N, 512)
             for k in range(PASSES):
-                codes, plane = w_slices(k, block)
                 for t in rows:
-                    part, at = (0, t * P) if t < 2 else (1, (t - 2) * P)
+                    (codes, plane), col = x_tile(t)
                     nc.tensor.matmul_mx(
                         out=banks[t][:],
-                        lhsT=x_codes[part][:, k, 2 * at : 2 * (at + P)].bitcast(FP4X4),
-                        lhsT_scale=x_planes[part][:, k, at : at + P],
-                        rhs=codes,
-                        rhs_scale=plane,
+                        lhsT=codes[:, k, 2 * col : 2 * (col + P)].bitcast(FP4X4),
+                        lhsT_scale=plane[:, k, col : col + P],
+                        rhs=w[seg][0][:, k, 2 * at : 2 * (at + N)].bitcast(FP4X4),
+                        rhs_scale=w[seg][1][:, k, at : at + N],
                         start=(k == 0),
                         stop=(k == PASSES - 1),
                     )
             for t in rows:
                 accs[t, block] = banks[t]
 
-        out_rows = out.rearrange("s f h d -> f s (h d)")
-        accs, squares, rstds, parts, pend = {}, {}, {}, {}, []
-
-        def add_bias(u):
+        def add_bias(u, i):
             t, c, a, n = u
-            h = work.tile([P, n], F32, name="h", tag="h", bufs=3)
-            for i in range(0, n, N):
-                bank = accs.pop((t, (c * CHUNK + a + i) // N))
-                nc.vector.tensor_tensor(out=h[:, i : i + N], in0=bank[:], in1=b_sb[c][:, a + i : a + i + N], op=ALU.add)
-            parts[u] = {"h": h}
+            if i == 0:
+                parts[u] = {"h": work.tile([P, n], F32, name="h", tag="h", bufs=3)}
+            bank = accs.pop((t, (c * CHUNK + a) // N + i))
+            cols = slice(i * N, (i + 1) * N)
+            nc.vector.tensor_tensor(out=parts[u]["h"][:, cols], in0=bank[:], in1=b_sb[c][:, a + i * N : a + (i + 1) * N], op=ALU.add)
 
         def square(u, index, count):
             t, n = u[0], u[3]
@@ -187,7 +217,7 @@ def tile_temporalattention_pa_kernel(
             if index == count - 2:
                 base = work.tile([P, 1], F32, name="base", tag="base", bufs=4)
                 scrap = work.tile([P, 8], F32, name="scrap", tag="scrap", bufs=4)
-                which = 1 if t == TILES - 1 else 0
+                which = 1 if t == LAST_TILE else 0
                 nc.scalar.activation(out=scrap[:, 0 : index + 1], in_=squares[t][:, 0 : index + 1], func=ACT.Identity, scale=1.0 / D, bias=eps[:, which : which + 1], accum_out=base[:])
                 rstds[t] = base
             if index == count - 1:
@@ -228,75 +258,94 @@ def tile_temporalattention_pa_kernel(
             else:
                 nc.gpsimd.tensor_scalar(out=v, in0=v, scalar1=rstd[:], scalar2=0.0, op0=ALU.mult, op1=ALU.add)
 
-        def store(u, a, n, queues):
-            t, c, first = u[:3]
-            for half in range(2):
-                queues[half].dma_start(
-                    out=out_rows[2 * t + half, :, c * CHUNK + first + a : c * CHUNK + first + a + n],
-                    in_=parts[u]["r"][64 * half : 64 * (half + 1), a : a + n],
-                )
+        out_rows = out.rearrange("s f h d -> f s (h d)")
+        out_last = out.rearrange("s (e f) h d -> f (s e) (h d)", e=2)
 
         def finish(u):
-            scale(u, 0, u[3], "s")
-            store(u, 0, u[3], (nc.sync, nc.sync))
+            t, c, a, n = u
+            scale(u, 0, n, "s")
+            for half in range(2):
+                nc.sync.dma_start(
+                    out=out_rows[TILE_FRAMES[t][half], :, c * CHUNK + a : c * CHUNK + a + n],
+                    in_=parts[u]["r"][64 * half : 64 * (half + 1), :],
+                )
 
-        spread_b(0, 0, "wp1", 1, nc.vector.tensor_copy)
-        spread_b(0, 1, "wp3", 1, nc.vector.tensor_copy)
-        spread_w(0, 0, "mx", 4, nc.scalar.copy)
-        spread_w(0, 1, "mx", 4, nc.scalar.copy)
-        spread_b(1, 0, "wp3", 1, nc.vector.tensor_copy)
-        spread_b(1, 1, "wp1", 1, nc.vector.tensor_copy)
-        jobs = [(table, 0), (table, 1)]
-        for c in range(1, CHUNKS):
-            for f in (spread_b, spread_w)[1 if c == 1 else 0 :]:
-                jobs += [(f, c, half, "wp3", 1, nc.scalar.copy) for half in range(2)]
-
-        def job():
-            if jobs:
-                f, *args = jobs.pop(0)
-                f(*args)
-
+        by_vector, by_scalar = nc.vector.tensor_copy, nc.scalar.copy
+        for c, tag, bufs in ((0, "mx", 4), (1, "tab", 2)):
+            spread_b(c, 0, tag, bufs, by_vector)
+            spread_b(c, 1, tag, bufs, by_scalar)
+        spread_w(1, 0, "", 1, None)
+        spread_w(1, 1, "", 1, None)
+        spread_w(3, 0, "", 1, None)
+        spread_w(3, 1, "", 1, None)
+        spread_w(0, 0, "mx", 4, by_vector)
+        spread_w(0, 1, "mx", 4, by_scalar)
+        for c, tag, bufs in ((2, "mx", 4), (3, "tab", 2)):
+            spread_b(c, 0, tag, bufs, by_vector)
+            spread_b(c, 1, tag, bufs, by_scalar)
+        spread_w(2, 0, "mx", 4, by_vector)
+        spread_w(2, 1, "mx", 4, by_scalar)
         engines = {"v": nc.vector, "g": nc.gpsimd}
-        steps = [(t, c, 0, CHUNK) for c in range(CHUNKS) for t in (0, 1)]
-        steps += [(t, c, 0, CHUNK) for t in range(2, TILES - 1) for c in range(CHUNKS)]
-        prev = None
-        for u in steps:
-            t, c = u[:2]
-            if t >= 2 and c == 1:
-                table(t)
-            for block in (2 * c, 2 * c + 1):
-                if (t, c) == (0, 0):
-                    mx((0, 1), block)
-                    for i in range(3):
-                        job()
-                elif (t, c) != (1, 0):
-                    mx((t,), block)
-                    job()
-            add_bias(u)
-            square(u, c, CHUNKS)
-            if prev:
-                turn(prev, 0)
-            gain(u, nc.vector if c in V_CHUNKS else nc.gpsimd)
-            if prev:
-                turn(prev, 1)
-                join(prev, nc.gpsimd)
-            for i in range(min(len(pend), 2 if pend and pend[0][0] < 2 else 1)):
-                finish(pend.pop(0))
-            if c == CHUNKS - 1:
-                pend.extend((t, cc, 0, CHUNK) for cc in range(CHUNKS))
-            prev = u
+        waiting = []
+        for c in range(CHUNKS):
+            us = [(t, c, 0, CHUNK) for t in (0, 1)]
+            for half in range(2):
+                mx((0, 1), 2 * c + half)
+                if (c, half) == (0, 0):
+                    table(0)
+                    table(1)
+                for u in us:
+                    add_bias(u, half)
+                if half == 1:
+                    for u in us:
+                        square(u, c, CHUNKS)
+                        gain(u, nc.vector if c in V_CHUNKS else nc.gpsimd)
+                if waiting:
+                    old = waiting.pop(0)
+                    turn(old, 0)
+                    turn(old, 1)
+                    join(old, nc.gpsimd)
+            waiting = us
+        pend = [(t, c, 0, CHUNK) for t in (0, 1) for c in range(CHUNKS)]
 
-        t = TILES - 1
+        for t in range(2, LAST_TILE):
+            for c in range(CHUNKS):
+                u = (t, c, 0, CHUNK)
+                for block in (2 * c, 2 * c + 1):
+                    mx((t,), block)
+                if c == 1:
+                    table(t)
+                for old in waiting[:-1]:
+                    turn(old, 0)
+                    turn(old, 1)
+                    join(old, nc.gpsimd)
+                old = waiting[-1]
+                add_bias(u, 0)
+                add_bias(u, 1)
+                square(u, c, CHUNKS)
+                turn(old, 0)
+                gain(u, nc.vector if c in V_CHUNKS else nc.gpsimd)
+                turn(old, 1)
+                join(old, nc.gpsimd)
+                waiting = [u]
+                for i in range(2 if pend[0][0] < 2 else 1):
+                    finish(pend.pop(0))
+                if c == 2 and 3 <= t < 7:
+                    interleave(t - 3)
+            pend.extend((t, c, 0, CHUNK) for c in range(CHUNKS))
+
+        t = LAST_TILE
         last = [(t,) + unit for unit in LAST]
         for i, u in enumerate(last):
-            if i == 1:
-                table(t)
             for block in range((u[1] * CHUNK + u[2]) // N, (u[1] * CHUNK + u[2] + u[3]) // N):
                 mx((t,), block)
+            if i == 1:
+                table(t)
         for what, i, engine in PLAN:
-            u = prev if i < 0 else last[i] if i < len(last) else None
+            u = waiting[0] if i < 0 else last[i] if i < len(last) else None
             if what == "b":
-                add_bias(u)
+                for j in range(u[3] // N):
+                    add_bias(u, j)
             elif what == "q":
                 square(u, i, len(last))
             elif what == "w":
@@ -310,5 +359,7 @@ def tile_temporalattention_pa_kernel(
             elif what == "f":
                 finish(pend.pop(0))
         for engine, i, a, n in TAIL:
-            scale(last[i], a, n, engine)
-            store(last[i], a, n, (nc.sync, nc.scalar))
+            u = last[i]
+            scale(u, a, n, engine)
+            first = u[1] * CHUNK + u[2] + a
+            nc.sync.dma_start(out=out_last[11, :, first : first + n], in_=parts[u]["r"][:, a : a + n])

@@ -45,8 +45,8 @@ def tile_temporalattention_pa_kernel(
         ctx.enter_context(tc.manual_schedule())
 
         def operand(name, cols):
-            codes = keep.tile([P, PASSES, 2 * cols], U8, name=name + "_codes", align_bytes=64)
-            plane = keep.tile([P, PASSES, cols], U8, name=name + "_plane", align_bytes=64)
+            codes = keep.tile([P, PASSES, 2 * cols], U8, name=name + "_codes", align_bytes=256)
+            plane = keep.tile([P, PASSES, cols], U8, name=name + "_plane", align_bytes=256)
             return codes, plane
 
         def load_codes(tile, at, words, first, count, k0, k1):
@@ -94,7 +94,7 @@ def tile_temporalattention_pa_kernel(
         zero(nc.gpsimd, x_high[1])
         zero(nc.gpsimd, x_low[1])
 
-        kx, kw, kw2 = 3, 3, 5
+        kx, kw, kw2 = 3, 4, 6
         load_codes(x_first[0], 0, x_words, 0, 256, 0, kx)
         load_codes(w[0][0], 0, w_words, 0, 512, 0, kw)
         load_scales(x_first[1], 0, x_scales, 0, 256)
@@ -212,7 +212,7 @@ def tile_temporalattention_pa_kernel(
             t, n = u[0], u[3]
             if index == 0:
                 squares[t] = work.tile([P, 8], F32, name="ss", tag="ss", bufs=4)
-            junk = work.tile([P, n], BF16, name="junk", tag="junk", bufs=2)
+            junk = work.tile([P, n], BF16, name="junk", tag="junk", bufs=1)
             nc.scalar.activation(out=junk[:], in_=parts[u]["h"][:], func=ACT.Square, accum_out=squares[t][:, index : index + 1])
             if index == count - 2:
                 base = work.tile([P, 1], F32, name="base", tag="base", bufs=4)

from contextlib import ExitStack

import concourse.mybir as mybir
from concourse.masks import make_identity

F32 = mybir.dt.float32
BF16 = mybir.dt.bfloat16
I32 = mybir.dt.int32
U8 = mybir.dt.uint8
FP4X4 = mybir.dt.float4_e2m1fn_x4
ACT = mybir.ActivationFunctionType
ALU = mybir.AluOpType

FRAMES, TOKENS, D, HEADS = 24, 64, 4096, 16
HEAD = D // HEADS
PAIRS = HEAD // 2
ROWS = FRAMES * TOKENS
EPS = 1e-6

P = 128
PASSES = D // 512
TILES = ROWS // P
N = 512
CHUNK = 1024
CHUNKS = D // CHUNK

FLOPS = 2 * ROWS * D * D

V_CHUNKS = (1, 3)
LAST_TILE = TILES - 1
TILE_FRAMES = [(0, 1), (2, 3), (13, 14), (15, 16), (17, 18), (19, 20), (21, 22), (4, 5), (6, 7), (8, 9), (10, 12), (11, 23)]
LAST = [(0, 0, 1024), (1, 0, 1024), (2, 0, 512), (2, 512, 512), (3, 0, 512), (3, 512, 512)]
PLAN = [("b", 0, ""), ("q", 0, ""), ("f", 99, ""), ("r", -1, ""), ("s", -1, ""), ("w", 0, "g"), ("j", -1, "g"), ("b", 1, ""), ("q", 1, ""), ("f", 99, ""), ("r", 0, ""), ("s", 0, ""), ("b", 2, ""), ("w", 1, "v"), ("b", 3, ""), ("q", 2, ""), ("q", 3, ""), ("r", 1, ""), ("s", 1, ""), ("j", 0, "g"), ("w", 2, "g"), ("w", 3, "g"), ("f", 99, ""), ("b", 4, ""), ("j", 1, "g"), ("f", 99, ""), ("r", 2, ""), ("s", 2, ""), ("b", 5, ""), ("q", 4, ""), ("q", 5, ""), ("w", 4, "v"), ("r", 3, ""), ("s", 3, ""), ("j", 2, "g"), ("w", 5, "v"), ("r", 4, ""), ("s", 4, ""), ("j", 3, "g"), ("j", 4, "g"), ("r", 5, ""), ("s", 5, ""), ("j", 5, "v")]
TAIL = [("s", 0, 0, 512), ("s", 0, 512, 512), ("s", 1, 0, 512), ("s", 1, 512, 512), ("s", 2, 0, 512), ("s", 3, 0, 512), ("v", 4, 0, 512), ("v", 5, 0, 512)]


def tile_temporalattention_pa_kernel(
    tc, x_words, x_scales, freqs_cos, freqs_sin, w_words, w_scales, proj_b, norm_w, out
):
    nc = tc.nc
    with ExitStack() as ctx:
        keep = ctx.enter_context(tc.tile_pool(name="keep", bufs=1))
        work = ctx.enter_context(tc.tile_pool(name="work", bufs=2))
        psum = ctx.enter_context(tc.psum_pool(name="psum", bufs=1))
        ctx.enter_context(tc.manual_schedule())

        def operand(name, cols):
            codes = keep.tile([P, PASSES, 2 * cols], U8, name=name + "_codes", align_bytes=256)
            plane = keep.tile([P, PASSES, cols], U8, name=name + "_plane", align_bytes=256)
            return codes, plane

        def load_codes(tile, at, words, first, count, k0, k1):
            nc.sync.dma_start(
                out=tile[:, k0:k1, 2 * at : 2 * (at + count)].bitcast(I32),
                in_=words[k0:k1, :, 2 * first : 2 * (first + count)].rearrange("g p n -> p g n").bitcast(I32),
            )

        def load_scales(tile, at, scales, first, count):
            for r in range(4):
                nc.sync.dma_start(
                    out=tile[r:P:32, :, at : at + count].bitcast(I32),
                    in_=scales[:, r:16:4, first : first + count].rearrange("g r n -> r g n").bitcast(I32),
                )

        def zero(engine, tile):
            engine.memset(tile[:].bitcast(I32), 0)

        x_first = operand("xa", 4 * TOKENS)
        x_high = operand("xb", 13 * TOKENS)
        x_low = operand("xc", 8 * TOKENS)
        x_last = operand("xd", 2 * TOKENS)
        w = [operand(f"w{i}", 512) for i in range(D // 512)]

        bw = keep.tile([P, N], BF16, name="bw")
        ident = keep.tile([P, P], BF16, name="ident")
        neg = keep.tile([P, P], BF16, name="neg")
        eps = keep.tile([P, 2], F32, name="eps")
        cs0 = keep.tile([P, 2, 2, PAIRS], BF16, name="cs0")
        cs1 = keep.tile([P, 2, TILES - 2, PAIRS], BF16, name="cs1")

        zero(nc.vector, bw)
        zero(nc.vector, x_first[1])
        zero(nc.vector, w[0][1])
        make_identity(nc, ident[:])
        nc.scalar.dma_start(out=bw[0:8, :], in_=proj_b.rearrange("(r n) -> r n", r=8))
        nc.scalar.dma_start(out=bw[8:16, :], in_=norm_w.rearrange("(r n) -> r n", r=8))
        for i, f in enumerate((freqs_cos, freqs_sin)):
            nc.gpsimd.dma_start(out=cs0[:, i, :, :], in_=f[0 : 2 * P, :].rearrange("(t p) j -> p t j", p=P))
        nc.vector.memset(eps[:, 0:1], EPS / (CHUNKS - 1))
        nc.vector.memset(eps[:, 1:2], EPS / (len(LAST) - 1))
        nc.scalar.activation(out=neg[:], in_=ident[:], func=ACT.Copy, scale=-1.0)
        for i in range(1, len(w)):
            zero(nc.gpsimd, w[i][1])
        zero(nc.gpsimd, x_high[1])
        zero(nc.gpsimd, x_low[1])

        kx, kw, kw2 = 3, 4, 6
        load_codes(x_first[0], 0, x_words, 0, 256, 0, kx)
        load_codes(w[0][0], 0, w_words, 0, 512, 0, kw)
        load_scales(x_first[1], 0, x_scales, 0, 256)
        load_scales(w[0][1], 0, w_scales, 0, 512)
        load_codes(x_first[0], 0, x_words, 0, 256, kx, PASSES)
        load_codes(w[0][0], 0, w_words, 0, 512, kw, kw2)
        load_codes(w[0][0], 0, w_words, 0, 512, kw2, PASSES)
        for i in range(1, len(w)):
            load_scales(w[i][1], 0, w_scales, i * 512, 512)
            load_codes(w[i][0], 0, w_words, i * 512, 512, 0, 4)
            load_codes(w[i][0], 0, w_words, i * 512, 512, 4, 8)
        load_scales(x_high[1], 0, x_scales, 11 * TOKENS, 13 * TOKENS)
        load_codes(x_high[0], 0, x_words, 11 * TOKENS, 13 * TOKENS, 0, 4)
        load_codes(x_high[0], 0, x_words, 11 * TOKENS, 13 * TOKENS, 4, 8)

        def load_tables(first, count, frame):
            for i, f in enumerate((freqs_cos, freqs_sin)):
                rows = f[frame * TOKENS : (frame + 2 * count) * TOKENS, :]
                nc.sync.dma_start(out=cs1[:, i, first : first + count, :], in_=rows.rearrange("(t p) j -> p t j", p=P))

        def load_half_table(tile, partitions, frame):
            for i, f in enumerate((freqs_cos, freqs_sin)):
                nc.sync.dma_start(out=cs1[partitions, i, tile, :], in_=f[frame * TOKENS : (frame + 1) * TOKENS, :])

        load_tables(0, 5, 13)
        for at, first, count in ((0, 4, 7), (7, 12, 1)):
            load_scales(x_low[1], at * TOKENS, x_scales, first * TOKENS, count * TOKENS)
            load_codes(x_low[0], at * TOKENS, x_words, first * TOKENS, count * TOKENS, 0, 8)
        load_tables(5, 3, 4)
        load_half_table(8, slice(0, 64), 10)
        load_half_table(8, slice(64, 128), 12)
        load_half_table(9, slice(0, 128, 2), 11)
        load_half_table(9, slice(1, 128, 2), 23)

        def interleave(piece):
            which, e = divmod(piece, 2)
            b = 2 if which == 0 else 1
            frame = 0 if e == 0 else 12
            nc.vector.tensor_copy(
                out=x_last[which][:].rearrange("p k (s e b) -> p k e s b", e=2, b=b)[:, :, e, :, :],
                in_=x_high[which][:, :, b * frame * TOKENS : b * (frame + 1) * TOKENS].rearrange("p k (s b) -> p k s b", b=b),
            )

        b_sb, w_sb = {}, {}
        for c in range(CHUNKS):
            b_sb[c] = keep.tile([P, CHUNK], BF16, name=f"b{c}")
            if c not in V_CHUNKS:
                w_sb[c] = keep.tile([P, CHUNK], F32, name=f"g{c}")

        def spread(dst, row):
            nc.tensor.matmul(dst, lhsT=ident[:, row : row + 1].to_broadcast([P, P]), rhs=bw[:], start=True, stop=True)

        def spread_b(c, half, tag, bufs, copy):
            bank = psum.tile([P, N], F32, name="bank", tag=tag, bufs=bufs)
            spread(bank[:], 2 * c + half)
            copy(out=b_sb[c][:, half * N : (half + 1) * N], in_=bank[:])

        def spread_w(c, half, tag, bufs, copy):
            if c in V_CHUNKS:
                if half == 0:
                    w_sb[c] = psum.tile([P, CHUNK], BF16, name=f"wp{c}", tag=f"wp{c}", bufs=1)
                spread(w_sb[c][:, half * N : (half + 1) * N], 8 + 2 * c + half)
            else:
                bank = psum.tile([P, N], F32, name="bank", tag=tag, bufs=bufs)
                spread(bank[:], 8 + 2 * c + half)
                copy(out=w_sb[c][:, half * N : (half + 1) * N], in_=bank[:])

        tabs = {}

        def table(t):
            tab = psum.tile([P, PAIRS, 3], F32, name="tab", tag="tab", bufs=2)
            cs, i = (cs0, t) if t < 2 else (cs1, t - 2)
            for slot, (m, which) in enumerate(((neg, 1), (ident, 0), (ident, 1))):
                nc.tensor.matmul(tab[:, :, slot], lhsT=m[:], rhs=cs[:, which, i, :], start=True, stop=True)
            tabs[t] = tab

        def x_tile(t):
            if t < 2:
                return x_first, t * P
            if t < 7:
                return x_high, (TILE_FRAMES[t][0] - 11) * TOKENS
            if t < LAST_TILE:
                return x_low, (t - 7) * P
            return x_last, 0

        accs, squares, rstds, parts, pend = {}, {}, {}, {}, []

        def mx(rows, block):
            banks = {t: psum.tile([P, N], F32, name="mx", tag="mx", bufs=4) for t in rows}
            seg, at = divmod(block * N, 512)
            for k in range(PASSES):
                for t in rows:
                    (codes, plane), col = x_tile(t)
                    nc.tensor.matmul_mx(
                        out=banks[t][:],
                        lhsT=codes[:, k, 2 * col : 2 * (col + P)].bitcast(FP4X4),
                        lhsT_scale=plane[:, k, col : col + P],
                        rhs=w[seg][0][:, k, 2 * at : 2 * (at + N)].bitcast(FP4X4),
                        rhs_scale=w[seg][1][:, k, at : at + N],
                        start=(k == 0),
                        stop=(k == PASSES - 1),
                    )
            for t in rows:
                accs[t, block] = banks[t]

        def add_bias(u, i):
            t, c, a, n = u
            if i == 0:
                parts[u] = {"h": work.tile([P, n], F32, name="h", tag="h", bufs=3)}
            bank = accs.pop((t, (c * CHUNK + a) // N + i))
            cols = slice(i * N, (i + 1) * N)
            nc.vector.tensor_tensor(out=parts[u]["h"][:, cols], in0=bank[:], in1=b_sb[c][:, a + i * N : a + (i + 1) * N], op=ALU.add)

        def square(u, index, count):
            t, n = u[0], u[3]
            if index == 0:
                squares[t] = work.tile([P, 8], F32, name="ss", tag="ss", bufs=4)
            junk = work.tile([P, n], BF16, name="junk", tag="junk", bufs=1)
            nc.scalar.activation(out=junk[:], in_=parts[u]["h"][:], func=ACT.Square, accum_out=squares[t][:, index : index + 1])
            if index == count - 2:
                base = work.tile([P, 1], F32, name="base", tag="base", bufs=4)
                scrap = work.tile([P, 8], F32, name="scrap", tag="scrap", bufs=4)
                which = 1 if t == LAST_TILE else 0
                nc.scalar.activation(out=scrap[:, 0 : index + 1], in_=squares[t][:, 0 : index + 1], func=ACT.Identity, scale=1.0 / D, bias=eps[:, which : which + 1], accum_out=base[:])
                rstds[t] = base
            if index == count - 1:
                rstd = work.tile([P, 1], F32, name="rstd", tag="rstd", bufs=4)
                nc.scalar.activation(out=rstd[:], in_=squares[t][:, index : index + 1], func=ACT.Abs_reciprocal_sqrt, scale=1.0 / D, bias=rstds[t][:])
                rstds[t] = rstd

        def gain(u, engine):
            t, c, a, n = u
            g = work.tile([P, n], F32, name="g", tag="g", bufs=3)
            engine.tensor_tensor(out=g[:], in0=parts[u]["h"][:], in1=w_sb[c][:, a : a + n], op=ALU.mult)
            parts[u]["g"] = g

        def turn(u, which):
            t, c, a, n = u
            heads = n // HEAD
            tag, bufs = (("r", 10), ("s", 2))[which]
            prod = work.tile([P, n], F32, name="prod", tag=tag, bufs=bufs)
            nc.vector.tensor_tensor(
                out=prod[:].rearrange("p (h j e) -> p h j e", h=heads, e=2),
                in0=parts[u]["g"][:].rearrange("p (h j e) -> p h j e", h=heads, e=2)[:, :, :, which : which + 1].to_broadcast([P, heads, PAIRS, 2]),
                in1=tabs[t][:, :, 1 - which : 3 - which].unsqueeze(1).to_broadcast([P, heads, PAIRS, 2]),
                op=ALU.mult,
            )
            parts[u][tag] = prod

        def join(u, engine):
            r, s = parts[u]["r"], parts[u]["s"]
            engine.tensor_tensor(out=r[:], in0=r[:], in1=s[:], op=ALU.add)

        def scale(u, a, n, engine):
            v = parts[u]["r"][:, a : a + n]
            rstd = rstds[u[0]]
            if engine == "s":
                nc.scalar.activation(out=v, in_=v, func=ACT.Copy, scale=rstd[:])
            elif engine == "v":
                nc.vector.tensor_scalar(out=v, in0=v, scalar1=rstd[:], scalar2=None, op0=ALU.mult)
            else:
                nc.gpsimd.tensor_scalar(out=v, in0=v, scalar1=rstd[:], scalar2=0.0, op0=ALU.mult, op1=ALU.add)

        out_rows = out.rearrange("s f h d -> f s (h d)")
        out_last = out.rearrange("s (e f) h d -> f (s e) (h d)", e=2)

        def finish(u):
            t, c, a, n = u
            scale(u, 0, n, "s")
            for half in range(2):
                nc.sync.dma_start(
                    out=out_rows[TILE_FRAMES[t][half], :, c * CHUNK + a : c * CHUNK + a + n],
                    in_=parts[u]["r"][64 * half : 64 * (half + 1), :],
                )

        by_vector, by_scalar = nc.vector.tensor_copy, nc.scalar.copy
        for c, tag, bufs in ((0, "mx", 4), (1, "tab", 2)):
            spread_b(c, 0, tag, bufs, by_vector)
            spread_b(c, 1, tag, bufs, by_scalar)
        spread_w(1, 0, "", 1, None)
        spread_w(1, 1, "", 1, None)
        spread_w(3, 0, "", 1, None)
        spread_w(3, 1, "", 1, None)
        spread_w(0, 0, "mx", 4, by_vector)
        spread_w(0, 1, "mx", 4, by_scalar)
        for c, tag, bufs in ((2, "mx", 4), (3, "tab", 2)):
            spread_b(c, 0, tag, bufs, by_vector)
            spread_b(c, 1, tag, bufs, by_scalar)
        spread_w(2, 0, "mx", 4, by_vector)
        spread_w(2, 1, "mx", 4, by_scalar)
        engines = {"v": nc.vector, "g": nc.gpsimd}
        waiting = []
        for c in range(CHUNKS):
            us = [(t, c, 0, CHUNK) for t in (0, 1)]
            for half in range(2):
                mx((0, 1), 2 * c + half)
                if (c, half) == (0, 0):
                    table(0)
                    table(1)
                for u in us:
                    add_bias(u, half)
                if half == 1:
                    for u in us:
                        square(u, c, CHUNKS)
                        gain(u, nc.vector if c in V_CHUNKS else nc.gpsimd)
                if waiting:
                    old = waiting.pop(0)
                    turn(old, 0)
                    turn(old, 1)
                    join(old, nc.gpsimd)
            waiting = us
        pend = [(t, c, 0, CHUNK) for t in (0, 1) for c in range(CHUNKS)]

        for t in range(2, LAST_TILE):
            for c in range(CHUNKS):
                u = (t, c, 0, CHUNK)
                for block in (2 * c, 2 * c + 1):
                    mx((t,), block)
                if c == 1:
                    table(t)
                for old in waiting[:-1]:
                    turn(old, 0)
                    turn(old, 1)
                    join(old, nc.gpsimd)
                old = waiting[-1]
                add_bias(u, 0)
                add_bias(u, 1)
                square(u, c, CHUNKS)
                turn(old, 0)
                gain(u, nc.vector if c in V_CHUNKS else nc.gpsimd)
                turn(old, 1)
                join(old, nc.gpsimd)
                waiting = [u]
                for i in range(2 if pend[0][0] < 2 else 1):
                    finish(pend.pop(0))
                if c == 2 and 3 <= t < 7:
                    interleave(t - 3)
            pend.extend((t, c, 0, CHUNK) for c in range(CHUNKS))

        t = LAST_TILE
        last = [(t,) + unit for unit in LAST]
        for i, u in enumerate(last):
            for block in range((u[1] * CHUNK + u[2]) // N, (u[1] * CHUNK + u[2] + u[3]) // N):
                mx((t,), block)
            if i == 1:
                table(t)
        for what, i, engine in PLAN:
            u = waiting[0] if i < 0 else last[i] if i < len(last) else None
            if what == "b":
                for j in range(u[3] // N):
                    add_bias(u, j)
            elif what == "q":
                square(u, i, len(last))
            elif what == "w":
                gain(u, engines[engine])
            elif what == "r":
                turn(u, 0)
            elif what == "s":
                turn(u, 1)
            elif what == "j":
                join(u, engines[engine])
            elif what == "f":
                finish(pend.pop(0))
        for engine, i, a, n in TAIL:
            u = last[i]
            scale(u, a, n, engine)
            first = u[1] * CHUNK + u[2] + a
            nc.sync.dma_start(out=out_last[11, :, first : first + n], in_=parts[u]["r"][:, a : a + n])
